import numpy as np
import ml_dtypes


def mxq(x, axis, fmt="e4m3"):
    dtype, down = {"e4m3": (ml_dtypes.float8_e4m3fn, 7), "e5m2": (ml_dtypes.float8_e5m2, 14)}[fmt]
    v = np.moveaxis(np.asarray(x, np.float32).astype(ml_dtypes.bfloat16).astype(np.float64), axis, -1)
    blocks = v.reshape(v.shape[:-1] + (-1, 32))
    amax = np.abs(blocks).max(-1, keepdims=True)
    byte = np.maximum(np.where(amax > 0, np.frexp(amax)[1] - 1 + 127, 0) - down, 1)
    scale = np.exp2(byte - 127.0)
    codes = (blocks / scale).astype(np.float32).astype(dtype).astype(np.float64)
    return np.moveaxis((codes * scale).reshape(v.shape), -1, axis)


WIDE = False


def mx_kscale(k):
    if not WIDE:
        return np.ones(k)
    levels = np.array([10, -10, 5, -5, 0])
    a = np.random.permutation(np.resize(levels, k // 512 * 4)).reshape(k // 512, 4)
    idx = np.arange(k)
    return np.exp2(a[idx // 512, idx % 128 // 32])


BF16 = ml_dtypes.bfloat16


def bf(x):
    return np.asarray(x, np.float32).astype(BF16)


def f64(x):
    return np.asarray(x).astype(np.float64)


B, T, D, A, H, E = 8, 1024, 1024, 512, 4, 2048
DH = A // H
EPS = 1e-5


def layernorm(v, w, b):
    mu = v.mean(-1, keepdims=True)
    var = np.square(v - mu).mean(-1, keepdims=True)
    return (v - mu) / np.sqrt(var + EPS) * w + b


def setup_inputs():
    s = mx_kscale(D)
    return {'x': bf(np.random.standard_normal((B, T, D))),
            'ln_w': bf((1.0 + 0.1 * np.random.standard_normal(D)) * s),
            'ln_b': bf(0.1 * np.random.standard_normal(D) * s),
            'q_w': bf(np.random.standard_normal((D, A)) * 1.5 / np.sqrt(D) / s[:, None]),
            'q_b': bf(np.random.standard_normal(A) * 0.3)}


def reference(x, ln_w, ln_b, q_w, q_b):
    xn = layernorm(f64(x), f64(ln_w), f64(ln_b))
    q = (mxq(xn, 2, 'e4m3') @ mxq(f64(q_w), 0, 'e4m3')) + f64(q_b)
    q = q.reshape(B, T, H, DH)
    e = np.exp(q - q.max(-1, keepdims=True))
    return (e / e.sum(-1, keepdims=True)).reshape(B, T, A)

@@ -1,0 +1,257 @@
+from contextlib import ExitStack
+
+import concourse.mybir as mybir
+from concourse.masks import make_identity
+
+F32 = mybir.dt.float32
+BF16 = mybir.dt.bfloat16
+U32 = mybir.dt.uint32
+U8 = mybir.dt.uint8
+FP8X4 = mybir.dt.float8_e4m3fn_x4
+ALU = mybir.AluOpType
+ACT = mybir.ActivationFunctionType
+AXIS = mybir.AxisListType
+
+P = 128
+PACK = 4
+TOKENS = 8 * 1024
+D = 1024
+A = 512
+HEADS = 4
+HEAD = A // HEADS
+CHUNKS = D // P
+PASSES = D // (P * PACK)
+TILES = 4
+GROUP = TILES * P
+GROUPS = TOKENS // GROUP
+BN_MAX = 512
+BN_PARTS = D // BN_MAX
+RUN = 4
+EPS = 1e-5
+LEAD = 4
+
+FLOPS = 2 * TOKENS * D * A
+
+
+def tile_efficientcrossattention_pa_t_kernel(tc, x, ln_w, ln_b, q_w, q_b, out):
+    nc = tc.nc
+    x_groups = x.flatten_outer_dims().rearrange("(g p j) k -> g p j k", p=P, j=TILES)
+    out_groups = out.flatten_outer_dims().rearrange("(g p j) a -> g p j a", p=P, j=TILES)
+
+    with ExitStack() as stack:
+        const = stack.enter_context(tc.tile_pool(name="const", bufs=1))
+        loads = stack.enter_context(tc.tile_pool(name="loads", bufs=4))
+        small = stack.enter_context(tc.tile_pool(name="small", bufs=4))
+        hats = stack.enter_context(tc.tile_pool(name="hats", bufs=2))
+        plane_pool = stack.enter_context(tc.tile_pool(name="plane_pool", bufs=2 * PASSES))
+        packed = stack.enter_context(tc.tile_pool(name="packed", bufs=2))
+        logit_pool = stack.enter_context(tc.tile_pool(name="logit_pool", bufs=2))
+        stores = stack.enter_context(tc.tile_pool(name="stores", bufs=3))
+        psum_t = stack.enter_context(tc.psum_pool(name="psum_t", bufs=PACK))
+        psum_q = stack.enter_context(tc.psum_pool(name="psum_q", bufs=TILES))
+        stack.enter_context(tc.manual_schedule())
+
+        ln_rows = const.tile([P, P], BF16)
+        nc.vector.memset(ln_rows[:], 0.0)
+        nc.sync.dma_start(out=ln_rows[0:CHUNKS, :], in_=ln_w.rearrange("(c p) -> c p", p=P))
+        nc.sync.dma_start(out=ln_rows[CHUNKS : 2 * CHUNKS, :], in_=ln_b.rearrange("(c p) -> c p", p=P))
+        bias_all = const.tile([P, A], BF16)
+        nc.scalar.dma_start(out=bias_all[:], in_=q_b.partition_broadcast(P))
+        w_rows = const.tile([P, CHUNKS, A], BF16)
+        nc.scalar.dma_start(out=w_rows[:], in_=q_w.rearrange("(c p) n -> p c n", p=P))
+
+        identity = const.tile([P, P], F32)
+        make_identity(nc, identity[:])
+        minus_half = const.tile([P, TILES], F32)
+        nc.gpsimd.memset(minus_half[:], -0.5)
+
+        ln_cols = const.tile([P, 2 * CHUNKS], F32)
+
+        def transpose_norm_constants():
+            ln_rows_f32 = const.tile([P, P], F32)
+            nc.vector.tensor_copy(out=ln_rows_f32[:], in_=ln_rows[:])
+            ln_bank = psum_t.tile([P, GROUP], F32, tag="xt")
+            nc.tensor.transpose(out=ln_bank[:, 0:P], in_=ln_rows_f32[:], identity=identity[:])
+            nc.vector.tensor_copy(out=ln_cols[:], in_=ln_bank[:, 0 : 2 * CHUNKS])
+
+        w_codes = const.tile([P, PASSES, A], U32, align_bytes=64)
+        w_scales = const.tile([P, PASSES, A], U8, align_bytes=64)
+
+        def quantise_weights():
+            w_grouped = const.tile([P, PASSES, A, PACK], BF16, align_bytes=64)
+            for s in range(PASSES):
+                nc.vector.tensor_copy(
+                    out=w_grouped[:, s].rearrange("p (c i) t -> p c t i", i=RUN),
+                    in_=w_rows[:, s * PACK : (s + 1) * PACK, :].rearrange("p t (c i) -> p c t i", i=RUN),
+                )
+            nc.vector.quantize_mx(
+                out=w_codes[:].rearrange("p s n -> p (s n)").bitcast(FP8X4),
+                scales=w_scales[:].rearrange("p s n -> p (s n)"),
+                in_=w_grouped[:].rearrange("p s n t -> p (s n t)"),
+            )
+
+        x_of, rstd_of, minus_mean_of, x_hat_of, planes_of = {}, {}, {}, {}, {}
+        codes_of, scales_of, acc_of, logits_of, minus_max_of, result_of, sums_of = {}, {}, {}, {}, {}, {}, {}
+
+        def load(g):
+            x_sb = loads.tile([P, TILES, D], BF16)
+            nc.sync.dma_start(out=x_sb[:], in_=x_groups[g])
+            x_of[g] = x_sb
+
+        def statistics(g):
+            x_sb = x_of[g]
+            stats = small.tile([P, TILES, BN_PARTS, 6], F32)
+            mean_var = small.tile([P, TILES, 2], F32)
+            for j in range(TILES):
+                for h in range(BN_PARTS):
+                    nc.vector.bn_stats(out=stats[:, j, h, :], in_=x_sb[:, j, h * BN_MAX : (h + 1) * BN_MAX])
+                nc.vector.bn_aggr(out=mean_var[:, j, :], in_=stats[:, j].rearrange("p h s -> p (h s)"))
+            var_eps = small.tile([P, TILES], F32)
+            nc.gpsimd.tensor_scalar(
+                out=var_eps[:], in0=mean_var[:, :, 1], scalar1=1.0, scalar2=EPS, op0=ALU.mult, op1=ALU.add
+            )
+            rstd = small.tile([P, TILES], F32)
+            nc.gpsimd.tensor_tensor(out=rstd[:], in0=var_eps[:], in1=minus_half[:], op=ALU.pow)
+            minus_mean = small.tile([P, TILES], F32)
+            nc.gpsimd.tensor_scalar(
+                out=minus_mean[:], in0=mean_var[:, :, 0], scalar1=-1.0, scalar2=0.0, op0=ALU.mult, op1=ALU.add
+            )
+            rstd_of[g] = rstd
+            minus_mean_of[g] = minus_mean
+
+        def normalise(g):
+            x_hat = hats.tile([P, TILES, D], F32)
+            for j in range(TILES):
+                nc.gpsimd.tensor_scalar(
+                    out=x_hat[:, j, :],
+                    in0=x_of[g][:, j, :],
+                    scalar1=minus_mean_of[g][:, j : j + 1],
+                    scalar2=rstd_of[g][:, j : j + 1],
+                    op0=ALU.add,
+                    op1=ALU.mult,
+                )
+            x_hat_of[g] = x_hat
+
+        def transpose_pass(g, s):
+            planes = plane_pool.tile([P, PACK, GROUP], BF16)
+            for t in range(PACK):
+                c = s * PACK + t
+                xt = psum_t.tile([P, GROUP], F32, tag="xt")
+                for j in range(TILES):
+                    nc.tensor.transpose(
+                        out=xt[:, j * P : (j + 1) * P],
+                        in_=x_hat_of[g][:, j, c * P : (c + 1) * P],
+                        identity=identity[:],
+                    )
+                nc.scalar.activation(
+                    out=planes[:, t, :],
+                    in_=xt[:],
+                    func=ACT.Identity,
+                    scale=ln_cols[:, c : c + 1],
+                    bias=ln_cols[:, CHUNKS + c : CHUNKS + c + 1],
+                )
+            planes_of[g, s] = planes
+
+        def quantise(g):
+            grouped = packed.tile([P, PASSES, GROUP, PACK], BF16, align_bytes=64)
+            codes = packed.tile([P, PASSES, GROUP], U32, align_bytes=64)
+            scales = packed.tile([P, PASSES, GROUP], U8, align_bytes=64)
+            for s in range(PASSES):
+                nc.vector.tensor_copy(
+                    out=grouped[:, s].rearrange("p (c i) t -> p c t i", i=RUN),
+                    in_=planes_of[g, s][:].rearrange("p t (c i) -> p c t i", i=RUN),
+                )
+            for s in range(PASSES):
+                nc.vector.quantize_mx(
+                    out=codes[:, s, :].bitcast(FP8X4),
+                    scales=scales[:, s, :],
+                    in_=grouped[:, s].rearrange("p w t -> p (w t)"),
+                )
+            codes_of[g] = codes
+            scales_of[g] = scales
+
+        def project(g):
+            for j in range(TILES):
+                acc = psum_q.tile([P, A], F32)
+                for s in range(PASSES):
+                    nc.tensor.matmul_mx(
+                        out=acc[:],
+                        lhsT=codes_of[g][:, s, j * P : (j + 1) * P].bitcast(FP8X4),
+                        lhsT_scale=scales_of[g][:, s, j * P : (j + 1) * P],
+                        rhs=w_codes[:, s, :].bitcast(FP8X4),
+                        rhs_scale=w_scales[:, s, :],
+                        start=(s == 0),
+                        stop=(s == PASSES - 1),
+                    )
+                acc_of[g, j] = acc
+
+        def add_bias_and_find_max(g):
+            logits = logit_pool.tile([P, TILES, A], F32)
+            for j in range(TILES):
+                nc.vector.tensor_tensor(out=logits[:, j, :], in0=acc_of[g, j][:], in1=bias_all[:], op=ALU.add)
+            minus_max = small.tile([P, TILES * HEADS], F32)
+            nc.vector.tensor_reduce(
+                out=minus_max[:],
+                in_=logits[:].rearrange("p j (h a) -> p (j h) a", a=HEAD),
+                axis=AXIS.X,
+                op=ALU.max,
+                negate=True,
+            )
+            logits_of[g] = logits
+            minus_max_of[g] = minus_max
+
+        def exponentials(g):
+            result = stores.tile([P, TILES, A], F32)
+            sums = small.tile([P, TILES * HEADS], F32)
+            for j in range(TILES):
+                for h in range(HEADS):
+                    n = j * HEADS + h
+                    nc.scalar.activation(
+                        out=result[:, j, h * HEAD : (h + 1) * HEAD],
+                        in_=logits_of[g][:, j, h * HEAD : (h + 1) * HEAD],
+                        func=ACT.Exp,
+                        bias=minus_max_of[g][:, n : n + 1],
+                        scale=1.0,
+                        accum_out=sums[:, n : n + 1],
+                    )
+            result_of[g] = result
+            sums_of[g] = sums
+
+        def divide_and_store(g):
+            result = result_of[g]
+            inv_sums = small.tile([P, TILES * HEADS], F32)
+            nc.vector.reciprocal(out=inv_sums[:], in_=sums_of[g][:])
+            for j in range(TILES):
+                for h in range(HEADS):
+                    n = j * HEADS + h
+                    nc.scalar.activation(
+                        out=result[:, j, h * HEAD : (h + 1) * HEAD],
+                        in_=result[:, j, h * HEAD : (h + 1) * HEAD],
+                        func=ACT.Copy,
+                        scale=inv_sums[:, n : n + 1],
+                    )
+            nc.sync.dma_start(out=out_groups[g], in_=result[:])
+
+        def run(stage, g, *more):
+            if 0 <= g < GROUPS:
+                stage(g, *more)
+
+        def step(i):
+            run(load, i + LEAD)
+            run(exponentials, i - 1)
+            run(transpose_pass, i + 1, 0)
+            run(quantise, i)
+            run(project, i)
+            run(transpose_pass, i + 1, 1)
+            run(normalise, i + 2)
+            run(statistics, i + 3)
+            run(divide_and_store, i - 1)
+            run(add_bias_and_find_max, i)
+
+        step(-LEAD)
+        step(1 - LEAD)
+        transpose_norm_constants()
+        step(2 - LEAD)
+        quantise_weights()
+        for i in range(3 - LEAD, GROUPS + 1):
+            step(i)

@@ -29,6 +29,7 @@ BN_PARTS = D // BN_MAX
 RUN = 4
 EPS = 1e-5
 LEAD = 4
+SCALAR_TILES = 2
 
 FLOPS = 2 * TOKENS * D * A
 
@@ -47,16 +48,16 @@ def tile_efficientcrossattention_pa_t_kernel(tc, x, ln_w, ln_b, q_w, q_b, out):
         packed = stack.enter_context(tc.tile_pool(name="packed", bufs=2))
         logit_pool = stack.enter_context(tc.tile_pool(name="logit_pool", bufs=2))
         stores = stack.enter_context(tc.tile_pool(name="stores", bufs=3))
-        psum_t = stack.enter_context(tc.psum_pool(name="psum_t", bufs=PACK))
-        psum_q = stack.enter_context(tc.psum_pool(name="psum_q", bufs=TILES))
+        psum_t = stack.enter_context(tc.psum_pool(name="psum_t", bufs=2))
+        psum_q = stack.enter_context(tc.psum_pool(name="psum_q", bufs=2))
+        psum_l = stack.enter_context(tc.psum_pool(name="psum_l", bufs=TILES))
         stack.enter_context(tc.manual_schedule())
 
         ln_rows = const.tile([P, P], BF16)
         nc.vector.memset(ln_rows[:], 0.0)
         nc.sync.dma_start(out=ln_rows[0:CHUNKS, :], in_=ln_w.rearrange("(c p) -> c p", p=P))
         nc.sync.dma_start(out=ln_rows[CHUNKS : 2 * CHUNKS, :], in_=ln_b.rearrange("(c p) -> c p", p=P))
-        bias_all = const.tile([P, A], BF16)
-        nc.scalar.dma_start(out=bias_all[:], in_=q_b.partition_broadcast(P))
+        nc.sync.dma_start(out=ln_rows[2 * CHUNKS : 2 * CHUNKS + HEADS, :], in_=q_b.rearrange("(h p) -> h p", p=P))
         w_rows = const.tile([P, CHUNKS, A], BF16)
         nc.scalar.dma_start(out=w_rows[:], in_=q_w.rearrange("(c p) n -> p c n", p=P))
 
@@ -65,14 +66,14 @@ def tile_efficientcrossattention_pa_t_kernel(tc, x, ln_w, ln_b, q_w, q_b, out):
         minus_half = const.tile([P, TILES], F32)
         nc.gpsimd.memset(minus_half[:], -0.5)
 
-        ln_cols = const.tile([P, 2 * CHUNKS], F32)
+        ln_cols = const.tile([P, 2 * CHUNKS + HEADS], F32)
 
         def transpose_norm_constants():
             ln_rows_f32 = const.tile([P, P], F32)
             nc.vector.tensor_copy(out=ln_rows_f32[:], in_=ln_rows[:])
             ln_bank = psum_t.tile([P, GROUP], F32, tag="xt")
             nc.tensor.transpose(out=ln_bank[:, 0:P], in_=ln_rows_f32[:], identity=identity[:])
-            nc.vector.tensor_copy(out=ln_cols[:], in_=ln_bank[:, 0 : 2 * CHUNKS])
+            nc.vector.tensor_copy(out=ln_cols[:], in_=ln_bank[:, 0 : 2 * CHUNKS + HEADS])
 
         w_codes = const.tile([P, PASSES, A], U32, align_bytes=64)
         w_scales = const.tile([P, PASSES, A], U8, align_bytes=64)
@@ -91,7 +92,7 @@ def tile_efficientcrossattention_pa_t_kernel(tc, x, ln_w, ln_b, q_w, q_b, out):
             )
 
         x_of, rstd_of, minus_mean_of, x_hat_of, planes_of = {}, {}, {}, {}, {}
-        codes_of, scales_of, acc_of, logits_of, minus_max_of, result_of, sums_of = {}, {}, {}, {}, {}, {}, {}
+        codes_of, scales_of, logits_t_of, logits_of, minus_max_of, result_of, sums_of = {}, {}, {}, {}, {}, {}, {}
 
         def load(g):
             x_sb = loads.tile([P, TILES, D], BF16)
@@ -171,66 +172,76 @@ def tile_efficientcrossattention_pa_t_kernel(tc, x, ln_w, ln_b, q_w, q_b, out):
             scales_of[g] = scales
 
         def project(g):
-            for j in range(TILES):
-                acc = psum_q.tile([P, A], F32)
+            logits_t = logit_pool.tile([P, HEADS, GROUP], F32)
+            for h in range(HEADS):
+                acc = psum_q.tile([P, GROUP], F32)
                 for s in range(PASSES):
                     nc.tensor.matmul_mx(
                         out=acc[:],
-                        lhsT=codes_of[g][:, s, j * P : (j + 1) * P].bitcast(FP8X4),
-                        lhsT_scale=scales_of[g][:, s, j * P : (j + 1) * P],
-                        rhs=w_codes[:, s, :].bitcast(FP8X4),
-                        rhs_scale=w_scales[:, s, :],
+                        lhsT=w_codes[:, s, h * HEAD : (h + 1) * HEAD].bitcast(FP8X4),
+                        lhsT_scale=w_scales[:, s, h * HEAD : (h + 1) * HEAD],
+                        rhs=codes_of[g][:, s, :].bitcast(FP8X4),
+                        rhs_scale=scales_of[g][:, s, :],
                         start=(s == 0),
                         stop=(s == PASSES - 1),
                     )
-                acc_of[g, j] = acc
+                nc.scalar.activation(
+                    out=logits_t[:, h, :],
+                    in_=acc[:],
+                    func=ACT.Identity,
+                    scale=1.0,
+                    bias=ln_cols[:, 2 * CHUNKS + h : 2 * CHUNKS + h + 1],
+                )
+            logits_t_of[g] = logits_t
 
-        def add_bias_and_find_max(g):
-            logits = logit_pool.tile([P, TILES, A], F32)
+        def transpose_back_and_find_max(g):
+            minus_max = small.tile([P, TILES, HEADS], F32)
             for j in range(TILES):
-                nc.vector.tensor_tensor(out=logits[:, j, :], in0=acc_of[g, j][:], in1=bias_all[:], op=ALU.add)
-            minus_max = small.tile([P, TILES * HEADS], F32)
-            nc.vector.tensor_reduce(
-                out=minus_max[:],
-                in_=logits[:].rearrange("p j (h a) -> p (j h) a", a=HEAD),
-                axis=AXIS.X,
-                op=ALU.max,
-                negate=True,
-            )
-            logits_of[g] = logits
+                logits = psum_l.tile([P, HEADS, HEAD], F32)
+                for h in range(HEADS):
+                    nc.tensor.transpose(
+                        out=logits[:, h, :], in_=logits_t_of[g][:, h, j * P : (j + 1) * P], identity=identity[:]
+                    )
+                nc.vector.tensor_reduce(out=minus_max[:, j, :], in_=logits[:], axis=AXIS.X, op=ALU.max, negate=True)
+                logits_of[g, j] = logits
             minus_max_of[g] = minus_max
 
         def exponentials(g):
-            result = stores.tile([P, TILES, A], F32)
-            sums = small.tile([P, TILES * HEADS], F32)
+            result = stores.tile([P, TILES, HEADS, HEAD], F32)
+            sums = small.tile([P, TILES, HEADS], F32)
             for j in range(TILES):
                 for h in range(HEADS):
-                    n = j * HEADS + h
                     nc.scalar.activation(
-                        out=result[:, j, h * HEAD : (h + 1) * HEAD],
-                        in_=logits_of[g][:, j, h * HEAD : (h + 1) * HEAD],
+                        out=result[:, j, h, :],
+                        in_=logits_of[g, j][:, h, :],
                         func=ACT.Exp,
-                        bias=minus_max_of[g][:, n : n + 1],
+                        bias=minus_max_of[g][:, j, h : h + 1],
                         scale=1.0,
-                        accum_out=sums[:, n : n + 1],
+                        accum_out=sums[:, j, h : h + 1],
                     )
             result_of[g] = result
             sums_of[g] = sums
 
         def divide_and_store(g):
             result = result_of[g]
-            inv_sums = small.tile([P, TILES * HEADS], F32)
+            inv_sums = small.tile([P, TILES, HEADS], F32)
             nc.vector.reciprocal(out=inv_sums[:], in_=sums_of[g][:])
             for j in range(TILES):
                 for h in range(HEADS):
-                    n = j * HEADS + h
-                    nc.scalar.activation(
-                        out=result[:, j, h * HEAD : (h + 1) * HEAD],
-                        in_=result[:, j, h * HEAD : (h + 1) * HEAD],
-                        func=ACT.Copy,
-                        scale=inv_sums[:, n : n + 1],
-                    )
-            nc.sync.dma_start(out=out_groups[g], in_=result[:])
+                    if j < SCALAR_TILES:
+                        nc.scalar.activation(
+                            out=result[:, j, h, :], in_=result[:, j, h, :], func=ACT.Copy, scale=inv_sums[:, j, h : h + 1]
+                        )
+                    else:
+                        nc.gpsimd.tensor_scalar(
+                            out=result[:, j, h, :],
+                            in0=result[:, j, h, :],
+                            scalar1=inv_sums[:, j, h : h + 1],
+                            scalar2=0.0,
+                            op0=ALU.mult,
+                            op1=ALU.add,
+                        )
+            nc.sync.dma_start(out=out_groups[g], in_=result[:].rearrange("p j h a -> p j (h a)"))
 
         def run(stage, g, *more):
             if 0 <= g < GROUPS:
@@ -244,9 +255,9 @@ def tile_efficientcrossattention_pa_t_kernel(tc, x, ln_w, ln_b, q_w, q_b, out):
             run(project, i)
             run(transpose_pass, i + 1, 1)
             run(normalise, i + 2)
-            run(statistics, i + 3)
             run(divide_and_store, i - 1)
-            run(add_bias_and_find_max, i)
+            run(statistics, i + 3)
+            run(transpose_back_and_find_max, i)
 
         step(-LEAD)
         step(1 - LEAD)

@@ -233,13 +233,12 @@ def tile_efficientcrossattention_pa_t_kernel(tc, x, ln_w, ln_b, q_w, q_b, out):
                             out=result[:, j, h, :], in_=result[:, j, h, :], func=ACT.Copy, scale=inv_sums[:, j, h : h + 1]
                         )
                     else:
-                        nc.gpsimd.tensor_scalar(
+                        nc.vector.tensor_scalar(
                             out=result[:, j, h, :],
                             in0=result[:, j, h, :],
                             scalar1=inv_sums[:, j, h : h + 1],
-                            scalar2=0.0,
+                            scalar2=None,
                             op0=ALU.mult,
-                            op1=ALU.add,
                         )
             nc.sync.dma_start(out=out_groups[g], in_=result[:].rearrange("p j h a -> p j (h a)"))
 

@@ -28,7 +28,6 @@ BN_MAX = 512
 BN_PARTS = D // BN_MAX
 RUN = 4
 EPS = 1e-5
-LEAD = 4
 SCALAR_TILES = 2
 
 FLOPS = 2 * TOKENS * D * A
@@ -43,11 +42,11 @@ def tile_efficientcrossattention_pa_t_kernel(tc, x, ln_w, ln_b, q_w, q_b, out):
         const = stack.enter_context(tc.tile_pool(name="const", bufs=1))
         loads = stack.enter_context(tc.tile_pool(name="loads", bufs=4))
         small = stack.enter_context(tc.tile_pool(name="small", bufs=4))
-        hats = stack.enter_context(tc.tile_pool(name="hats", bufs=2))
+        hats = stack.enter_context(tc.tile_pool(name="hats", bufs=3))
         plane_pool = stack.enter_context(tc.tile_pool(name="plane_pool", bufs=2 * PASSES))
-        packed = stack.enter_context(tc.tile_pool(name="packed", bufs=2))
-        logit_pool = stack.enter_context(tc.tile_pool(name="logit_pool", bufs=2))
-        stores = stack.enter_context(tc.tile_pool(name="stores", bufs=3))
+        packed = stack.enter_context(tc.tile_pool(name="packed", bufs=3))
+        logit_pool = stack.enter_context(tc.tile_pool(name="logit_pool", bufs=3))
+        stores = stack.enter_context(tc.tile_pool(name="stores", bufs=4))
         psum_t = stack.enter_context(tc.psum_pool(name="psum_t", bufs=2))
         psum_q = stack.enter_context(tc.psum_pool(name="psum_q", bufs=2))
         psum_l = stack.enter_context(tc.psum_pool(name="psum_l", bufs=TILES))
@@ -91,22 +90,26 @@ def tile_efficientcrossattention_pa_t_kernel(tc, x, ln_w, ln_b, q_w, q_b, out):
                 in_=w_grouped[:].rearrange("p s n t -> p (s n t)"),
             )
 
-        x_of, rstd_of, minus_mean_of, x_hat_of, planes_of = {}, {}, {}, {}, {}
-        codes_of, scales_of, logits_t_of, logits_of, minus_max_of, result_of, sums_of = {}, {}, {}, {}, {}, {}, {}
+        x_of, stats_of, mean_var_of, rstd_of, minus_mean_of, x_hat_of, planes_of, grouped_of = {}, {}, {}, {}, {}, {}, {}, {}
+        codes_of, scales_of, logits_t_of, logits_of, minus_max_of, result_of, sums_of, inv_of = {}, {}, {}, {}, {}, {}, {}, {}
 
         def load(g):
             x_sb = loads.tile([P, TILES, D], BF16)
             nc.sync.dma_start(out=x_sb[:], in_=x_groups[g])
             x_of[g] = x_sb
 
-        def statistics(g):
-            x_sb = x_of[g]
-            stats = small.tile([P, TILES, BN_PARTS, 6], F32)
-            mean_var = small.tile([P, TILES, 2], F32)
-            for j in range(TILES):
-                for h in range(BN_PARTS):
-                    nc.vector.bn_stats(out=stats[:, j, h, :], in_=x_sb[:, j, h * BN_MAX : (h + 1) * BN_MAX])
-                nc.vector.bn_aggr(out=mean_var[:, j, :], in_=stats[:, j].rearrange("p h s -> p (h s)"))
+        def statistics(g, j):
+            if j == 0:
+                stats = small.tile([P, TILES, BN_PARTS, 6], F32)
+                mean_var = small.tile([P, TILES, 2], F32)
+                stats_of[g] = stats
+                mean_var_of[g] = mean_var
+            for h in range(BN_PARTS):
+                nc.vector.bn_stats(out=stats_of[g][:, j, h, :], in_=x_of[g][:, j, h * BN_MAX : (h + 1) * BN_MAX])
+            nc.vector.bn_aggr(out=mean_var_of[g][:, j, :], in_=stats_of[g][:, j].rearrange("p h s -> p (h s)"))
+
+        def token_scalars(g):
+            mean_var = mean_var_of[g]
             var_eps = small.tile([P, TILES], F32)
             nc.gpsimd.tensor_scalar(
                 out=var_eps[:], in0=mean_var[:, :, 1], scalar1=1.0, scalar2=EPS, op0=ALU.mult, op1=ALU.add
@@ -120,148 +123,182 @@ def tile_efficientcrossattention_pa_t_kernel(tc, x, ln_w, ln_b, q_w, q_b, out):
             rstd_of[g] = rstd
             minus_mean_of[g] = minus_mean
 
-        def normalise(g):
-            x_hat = hats.tile([P, TILES, D], F32)
+        def normalise(g, j):
+            if j == 0:
+                x_hat = hats.tile([P, TILES, D], F32)
+                x_hat_of[g] = x_hat
+            nc.gpsimd.tensor_scalar(
+                out=x_hat_of[g][:, j, :],
+                in0=x_of[g][:, j, :],
+                scalar1=minus_mean_of[g][:, j : j + 1],
+                scalar2=rstd_of[g][:, j : j + 1],
+                op0=ALU.add,
+                op1=ALU.mult,
+            )
+
+        def transpose_chunk(g, c):
+            s, t = divmod(c, PACK)
+            if t == 0:
+                planes = plane_pool.tile([P, PACK, GROUP], BF16)
+                planes_of[g, s] = planes
+            xt = psum_t.tile([P, GROUP], F32, tag="xt")
             for j in range(TILES):
-                nc.gpsimd.tensor_scalar(
-                    out=x_hat[:, j, :],
-                    in0=x_of[g][:, j, :],
-                    scalar1=minus_mean_of[g][:, j : j + 1],
-                    scalar2=rstd_of[g][:, j : j + 1],
-                    op0=ALU.add,
-                    op1=ALU.mult,
+                nc.tensor.transpose(
+                    out=xt[:, j * P : (j + 1) * P],
+                    in_=x_hat_of[g][:, j, c * P : (c + 1) * P],
+                    identity=identity[:],
                 )
-            x_hat_of[g] = x_hat
+            nc.scalar.activation(
+                out=planes_of[g, s][:, t, :],
+                in_=xt[:],
+                func=ACT.Identity,
+                scale=ln_cols[:, c : c + 1],
+                bias=ln_cols[:, CHUNKS + c : CHUNKS + c + 1],
+            )
 
-        def transpose_pass(g, s):
-            planes = plane_pool.tile([P, PACK, GROUP], BF16)
-            for t in range(PACK):
-                c = s * PACK + t
-                xt = psum_t.tile([P, GROUP], F32, tag="xt")
-                for j in range(TILES):
-                    nc.tensor.transpose(
-                        out=xt[:, j * P : (j + 1) * P],
-                        in_=x_hat_of[g][:, j, c * P : (c + 1) * P],
-                        identity=identity[:],
-                    )
-                nc.scalar.activation(
-                    out=planes[:, t, :],
-                    in_=xt[:],
-                    func=ACT.Identity,
-                    scale=ln_cols[:, c : c + 1],
-                    bias=ln_cols[:, CHUNKS + c : CHUNKS + c + 1],
-                )
-            planes_of[g, s] = planes
+        def regroup(g, s):
+            grouped = packed.tile([P, GROUP, PACK], BF16, align_bytes=64)
+            nc.vector.tensor_copy(
+                out=grouped[:].rearrange("p (c i) t -> p c t i", i=RUN),
+                in_=planes_of[g, s][:].rearrange("p t (c i) -> p c t i", i=RUN),
+            )
+            grouped_of[g, s] = grouped
 
-        def quantise(g):
-            grouped = packed.tile([P, PASSES, GROUP, PACK], BF16, align_bytes=64)
-            codes = packed.tile([P, PASSES, GROUP], U32, align_bytes=64)
-            scales = packed.tile([P, PASSES, GROUP], U8, align_bytes=64)
+        def quantise(g, s):
+            if s == 0:
+                codes = packed.tile([P, PASSES, GROUP], U32, align_bytes=64)
+                scales = packed.tile([P, PASSES, GROUP], U8, align_bytes=64)
+                codes_of[g] = codes
+                scales_of[g] = scales
+            nc.vector.quantize_mx(
+                out=codes_of[g][:, s, :].bitcast(FP8X4),
+                scales=scales_of[g][:, s, :],
+                in_=grouped_of[g, s][:].rearrange("p w t -> p (w t)"),
+            )
+
+        def project(g, h):
+            if h == 0:
+                logits_t = logit_pool.tile([P, HEADS, GROUP], F32)
+                logits_t_of[g] = logits_t
+            acc = psum_q.tile([P, GROUP], F32)
             for s in range(PASSES):
-                nc.vector.tensor_copy(
-                    out=grouped[:, s].rearrange("p (c i) t -> p c t i", i=RUN),
-                    in_=planes_of[g, s][:].rearrange("p t (c i) -> p c t i", i=RUN),
+                nc.tensor.matmul_mx(
+                    out=acc[:],
+                    lhsT=w_codes[:, s, h * HEAD : (h + 1) * HEAD].bitcast(FP8X4),
+                    lhsT_scale=w_scales[:, s, h * HEAD : (h + 1) * HEAD],
+                    rhs=codes_of[g][:, s, :].bitcast(FP8X4),
+                    rhs_scale=scales_of[g][:, s, :],
+                    start=(s == 0),
+                    stop=(s == PASSES - 1),
                 )
-            for s in range(PASSES):
-                nc.vector.quantize_mx(
-                    out=codes[:, s, :].bitcast(FP8X4),
-                    scales=scales[:, s, :],
-                    in_=grouped[:, s].rearrange("p w t -> p (w t)"),
-                )
-            codes_of[g] = codes
-            scales_of[g] = scales
+            nc.scalar.activation(
+                out=logits_t_of[g][:, h, :],
+                in_=acc[:],
+                func=ACT.Identity,
+                scale=1.0,
+                bias=ln_cols[:, 2 * CHUNKS + h : 2 * CHUNKS + h + 1],
+            )
 
-        def project(g):
-            logits_t = logit_pool.tile([P, HEADS, GROUP], F32)
+        def transpose_back(g, j):
+            logits = psum_l.tile([P, HEADS, HEAD], F32)
             for h in range(HEADS):
-                acc = psum_q.tile([P, GROUP], F32)
-                for s in range(PASSES):
-                    nc.tensor.matmul_mx(
-                        out=acc[:],
-                        lhsT=w_codes[:, s, h * HEAD : (h + 1) * HEAD].bitcast(FP8X4),
-                        lhsT_scale=w_scales[:, s, h * HEAD : (h + 1) * HEAD],
-                        rhs=codes_of[g][:, s, :].bitcast(FP8X4),
-                        rhs_scale=scales_of[g][:, s, :],
-                        start=(s == 0),
-                        stop=(s == PASSES - 1),
-                    )
-                nc.scalar.activation(
-                    out=logits_t[:, h, :],
-                    in_=acc[:],
-                    func=ACT.Identity,
-                    scale=1.0,
-                    bias=ln_cols[:, 2 * CHUNKS + h : 2 * CHUNKS + h + 1],
+                nc.tensor.transpose(
+                    out=logits[:, h, :], in_=logits_t_of[g][:, h, j * P : (j + 1) * P], identity=identity[:]
                 )
-            logits_t_of[g] = logits_t
+            logits_of[g, j] = logits
 
-        def transpose_back_and_find_max(g):
-            minus_max = small.tile([P, TILES, HEADS], F32)
-            for j in range(TILES):
-                logits = psum_l.tile([P, HEADS, HEAD], F32)
-                for h in range(HEADS):
-                    nc.tensor.transpose(
-                        out=logits[:, h, :], in_=logits_t_of[g][:, h, j * P : (j + 1) * P], identity=identity[:]
-                    )
-                nc.vector.tensor_reduce(out=minus_max[:, j, :], in_=logits[:], axis=AXIS.X, op=ALU.max, negate=True)
-                logits_of[g, j] = logits
-            minus_max_of[g] = minus_max
+        def find_max(g, j):
+            if j == 0:
+                minus_max = small.tile([P, TILES, HEADS], F32)
+                minus_max_of[g] = minus_max
+            nc.vector.tensor_reduce(
+                out=minus_max_of[g][:, j, :], in_=logits_of[g, j][:], axis=AXIS.X, op=ALU.max, negate=True
+            )
 
-        def exponentials(g):
-            result = stores.tile([P, TILES, HEADS, HEAD], F32)
-            sums = small.tile([P, TILES, HEADS], F32)
-            for j in range(TILES):
-                for h in range(HEADS):
-                    nc.scalar.activation(
-                        out=result[:, j, h, :],
-                        in_=logits_of[g, j][:, h, :],
-                        func=ACT.Exp,
-                        bias=minus_max_of[g][:, j, h : h + 1],
-                        scale=1.0,
-                        accum_out=sums[:, j, h : h + 1],
-                    )
-            result_of[g] = result
-            sums_of[g] = sums
+        def exponentials(g, j):
+            if j == 0:
+                result = stores.tile([P, TILES, HEADS, HEAD], F32)
+                sums = small.tile([P, TILES, HEADS], F32)
+                result_of[g] = result
+                sums_of[g] = sums
+            for h in range(HEADS):
+                nc.scalar.activation(
+                    out=result_of[g][:, j, h, :],
+                    in_=logits_of[g, j][:, h, :],
+                    func=ACT.Exp,
+                    bias=minus_max_of[g][:, j, h : h + 1],
+                    scale=1.0,
+                    accum_out=sums_of[g][:, j, h : h + 1],
+                )
 
-        def divide_and_store(g):
-            result = result_of[g]
+        def invert_sums(g):
             inv_sums = small.tile([P, TILES, HEADS], F32)
             nc.vector.reciprocal(out=inv_sums[:], in_=sums_of[g][:])
-            for j in range(TILES):
-                for h in range(HEADS):
-                    if j < SCALAR_TILES:
-                        nc.scalar.activation(
-                            out=result[:, j, h, :], in_=result[:, j, h, :], func=ACT.Copy, scale=inv_sums[:, j, h : h + 1]
-                        )
-                    else:
-                        nc.vector.tensor_scalar(
-                            out=result[:, j, h, :],
-                            in0=result[:, j, h, :],
-                            scalar1=inv_sums[:, j, h : h + 1],
-                            scalar2=None,
-                            op0=ALU.mult,
-                        )
-            nc.sync.dma_start(out=out_groups[g], in_=result[:].rearrange("p j h a -> p j (h a)"))
+            inv_of[g] = inv_sums
 
-        def run(stage, g, *more):
+        def divide(g, j):
+            result = result_of[g]
+            for h in range(HEADS):
+                if j < SCALAR_TILES:
+                    nc.scalar.activation(
+                        out=result[:, j, h, :], in_=result[:, j, h, :], func=ACT.Copy, scale=inv_of[g][:, j, h : h + 1]
+                    )
+                else:
+                    nc.gpsimd.tensor_scalar(
+                        out=result[:, j, h, :],
+                        in0=result[:, j, h, :],
+                        scalar1=inv_of[g][:, j, h : h + 1],
+                        scalar2=0.0,
+                        op0=ALU.mult,
+                        op1=ALU.add,
+                    )
+
+        def store(g):
+            nc.sync.dma_start(out=out_groups[g], in_=result_of[g][:].rearrange("p j h a -> p j (h a)"))
+
+        def piece(stage, index):
+            g, r = divmod(index, TILES)
             if 0 <= g < GROUPS:
-                stage(g, *more)
+                stage(g, r)
 
-        def step(i):
-            run(load, i + LEAD)
-            run(exponentials, i - 1)
-            run(transpose_pass, i + 1, 0)
-            run(quantise, i)
-            run(project, i)
-            run(transpose_pass, i + 1, 1)
-            run(normalise, i + 2)
-            run(divide_and_store, i - 1)
-            run(statistics, i + 3)
-            run(transpose_back_and_find_max, i)
+        def whole(stage, index):
+            g, r = divmod(index, TILES)
+            if r == 0 and 0 <= g < GROUPS:
+                stage(g)
 
-        step(-LEAD)
-        step(1 - LEAD)
-        transpose_norm_constants()
-        step(2 - LEAD)
-        quantise_weights()
-        for i in range(3 - LEAD, GROUPS + 1):
-            step(i)
+        def two_chunks(g, r):
+            transpose_chunk(g, 2 * r)
+            transpose_chunk(g, 2 * r + 1)
+
+        def regroup_or_quantise(g, r):
+            if r % 2 == 0:
+                regroup(g, r // 2)
+            else:
+                quantise(g, r // 2)
+
+        def divide_two(g, r):
+            if r < SCALAR_TILES:
+                divide(g, r)
+                divide(g, r + SCALAR_TILES)
+
+        def tick(t):
+            whole(load, t + 13)
+            piece(two_chunks, t)
+            piece(project, t - 8)
+            piece(transpose_back, t - 12)
+            piece(find_max, t - 13)
+            piece(regroup_or_quantise, t - 3)
+            whole(invert_sums, t - 18)
+            piece(statistics, t + 9)
+            piece(exponentials, t - 14)
+            whole(token_scalars, t + 5)
+            piece(normalise, t + 5)
+            piece(divide_two, t - 19)
+            whole(store, t - 21)
+
+        for t in range(-13, 4 * (GROUPS - 1) + 22):
+            tick(t)
+            if t == -6:
+                transpose_norm_constants()
+            if t == -2:
+                quantise_weights()

@@ -35,12 +35,12 @@ FLOPS = 2 * TOKENS * D * A
 
 def tile_efficientcrossattention_pa_t_kernel(tc, x, ln_w, ln_b, q_w, q_b, out):
     nc = tc.nc
-    x_groups = x.flatten_outer_dims().rearrange("(g p j) k -> g p j k", p=P, j=TILES)
-    out_groups = out.flatten_outer_dims().rearrange("(g p j) a -> g p j a", p=P, j=TILES)
+    x_groups = x.flatten_outer_dims().rearrange("(g j p) k -> g j p k", p=P, j=TILES)
+    out_groups = out.flatten_outer_dims().rearrange("(g j p) a -> g j p a", p=P, j=TILES)
 
     with ExitStack() as stack:
         const = stack.enter_context(tc.tile_pool(name="const", bufs=1))
-        loads = stack.enter_context(tc.tile_pool(name="loads", bufs=4))
+        loads = stack.enter_context(tc.tile_pool(name="loads", bufs=5))
         small = stack.enter_context(tc.tile_pool(name="small", bufs=4))
         hats = stack.enter_context(tc.tile_pool(name="hats", bufs=3))
         plane_pool = stack.enter_context(tc.tile_pool(name="plane_pool", bufs=2 * PASSES))
@@ -93,10 +93,11 @@ def tile_efficientcrossattention_pa_t_kernel(tc, x, ln_w, ln_b, q_w, q_b, out):
         x_of, stats_of, mean_var_of, rstd_of, minus_mean_of, x_hat_of, planes_of, grouped_of = {}, {}, {}, {}, {}, {}, {}, {}
         codes_of, scales_of, logits_t_of, logits_of, minus_max_of, result_of, sums_of, inv_of = {}, {}, {}, {}, {}, {}, {}, {}
 
-        def load(g):
-            x_sb = loads.tile([P, TILES, D], BF16)
-            nc.sync.dma_start(out=x_sb[:], in_=x_groups[g])
-            x_of[g] = x_sb
+        def load(g, j):
+            if j == 0:
+                x_sb = loads.tile([P, TILES, D], BF16)
+                x_of[g] = x_sb
+            nc.scalar.dma_start(out=x_of[g][:, j, :], in_=x_groups[g, j])
 
         def statistics(g, j):
             if j == 0:
@@ -253,8 +254,8 @@ def tile_efficientcrossattention_pa_t_kernel(tc, x, ln_w, ln_b, q_w, q_b, out):
                         op1=ALU.add,
                     )
 
-        def store(g):
-            nc.sync.dma_start(out=out_groups[g], in_=result_of[g][:].rearrange("p j h a -> p j (h a)"))
+        def store(g, j):
+            nc.sync.dma_start(out=out_groups[g, j], in_=result_of[g][:, j].rearrange("p h a -> p (h a)"))
 
         def piece(stage, index):
             g, r = divmod(index, TILES)
@@ -281,8 +282,13 @@ def tile_efficientcrossattention_pa_t_kernel(tc, x, ln_w, ln_b, q_w, q_b, out):
                 divide(g, r)
                 divide(g, r + SCALAR_TILES)
 
+        def store_two(g, r):
+            if r < SCALAR_TILES:
+                store(g, r)
+                store(g, r + SCALAR_TILES)
+
         def tick(t):
-            whole(load, t + 13)
+            piece(load, t + 13)
             piece(two_chunks, t)
             piece(project, t - 8)
             piece(transpose_back, t - 12)
@@ -294,7 +300,7 @@ def tile_efficientcrossattention_pa_t_kernel(tc, x, ln_w, ln_b, q_w, q_b, out):
             whole(token_scalars, t + 5)
             piece(normalise, t + 5)
             piece(divide_two, t - 19)
-            whole(store, t - 21)
+            piece(store_two, t - 20)
 
         for t in range(-13, 4 * (GROUPS - 1) + 22):
             tick(t)

@@ -28,7 +28,7 @@ BN_MAX = 512
 BN_PARTS = D // BN_MAX
 RUN = 4
 EPS = 1e-5
-SCALAR_TILES = 2
+SCALAR_TILES = 4
 
 FLOPS = 2 * TOKENS * D * A
 
@@ -299,10 +299,10 @@ def tile_efficientcrossattention_pa_t_kernel(tc, x, ln_w, ln_b, q_w, q_b, out):
             piece(exponentials, t - 14)
             whole(token_scalars, t + 5)
             piece(normalise, t + 5)
-            piece(divide_two, t - 19)
-            piece(store_two, t - 20)
+            piece(divide, t - 19)
+            piece(store, t - 20)
 
-        for t in range(-13, 4 * (GROUPS - 1) + 22):
+        for t in range(-13, 4 * (GROUPS - 1) + 24):
             tick(t)
             if t == -6:
                 transpose_norm_constants()

@@ -28,7 +28,6 @@ BN_MAX = 512
 BN_PARTS = D // BN_MAX
 RUN = 4
 EPS = 1e-5
-SCALAR_TILES = 4
 
 FLOPS = 2 * TOKENS * D * A
 
@@ -58,7 +57,6 @@ def tile_efficientcrossattention_pa_t_kernel(tc, x, ln_w, ln_b, q_w, q_b, out):
         nc.sync.dma_start(out=ln_rows[CHUNKS : 2 * CHUNKS, :], in_=ln_b.rearrange("(c p) -> c p", p=P))
         nc.sync.dma_start(out=ln_rows[2 * CHUNKS : 2 * CHUNKS + HEADS, :], in_=q_b.rearrange("(h p) -> h p", p=P))
         w_rows = const.tile([P, CHUNKS, A], BF16)
-        nc.scalar.dma_start(out=w_rows[:], in_=q_w.rearrange("(c p) n -> p c n", p=P))
 
         identity = const.tile([P, P], F32)
         make_identity(nc, identity[:])
@@ -90,6 +88,7 @@ def tile_efficientcrossattention_pa_t_kernel(tc, x, ln_w, ln_b, q_w, q_b, out):
                 in_=w_grouped[:].rearrange("p s n t -> p (s n t)"),
             )
 
+        shift_of, var_eps_of = {}, {}
         x_of, stats_of, mean_var_of, rstd_of, minus_mean_of, x_hat_of, planes_of, grouped_of = {}, {}, {}, {}, {}, {}, {}, {}
         codes_of, scales_of, logits_t_of, logits_of, minus_max_of, result_of, sums_of, inv_of = {}, {}, {}, {}, {}, {}, {}, {}
 
@@ -107,35 +106,56 @@ def tile_efficientcrossattention_pa_t_kernel(tc, x, ln_w, ln_b, q_w, q_b, out):
                 mean_var_of[g] = mean_var
             for h in range(BN_PARTS):
                 nc.vector.bn_stats(out=stats_of[g][:, j, h, :], in_=x_of[g][:, j, h * BN_MAX : (h + 1) * BN_MAX])
-            nc.vector.bn_aggr(out=mean_var_of[g][:, j, :], in_=stats_of[g][:, j].rearrange("p h s -> p (h s)"))
+            if j % 2 == 1:
+                for i in (j - 1, j):
+                    nc.vector.bn_aggr(out=mean_var_of[g][:, i, :], in_=stats_of[g][:, i].rearrange("p h s -> p (h s)"))
 
-        def token_scalars(g):
+        def token_scalars(g, half):
+            if half == 0:
+                var_eps = small.tile([P, TILES], F32)
+                rstd = small.tile([P, TILES], F32)
+                minus_mean = small.tile([P, TILES], F32)
+                var_eps_of[g] = var_eps
+                rstd_of[g] = rstd
+                minus_mean_of[g] = minus_mean
+                if g == 0:
+                    shift = small.tile([P, TILES], F32)
+                    shift_of[g] = shift
+            pair = slice(2 * half, 2 * half + 2)
             mean_var = mean_var_of[g]
-            var_eps = small.tile([P, TILES], F32)
             nc.gpsimd.tensor_scalar(
-                out=var_eps[:], in0=mean_var[:, :, 1], scalar1=1.0, scalar2=EPS, op0=ALU.mult, op1=ALU.add
+                out=var_eps_of[g][:, pair], in0=mean_var[:, pair, 1], scalar1=1.0, scalar2=EPS, op0=ALU.mult, op1=ALU.add
             )
-            rstd = small.tile([P, TILES], F32)
-            nc.gpsimd.tensor_tensor(out=rstd[:], in0=var_eps[:], in1=minus_half[:], op=ALU.pow)
-            minus_mean = small.tile([P, TILES], F32)
+            nc.gpsimd.tensor_tensor(out=rstd_of[g][:, pair], in0=var_eps_of[g][:, pair], in1=minus_half[:, pair], op=ALU.pow)
             nc.gpsimd.tensor_scalar(
-                out=minus_mean[:], in0=mean_var[:, :, 0], scalar1=-1.0, scalar2=0.0, op0=ALU.mult, op1=ALU.add
+                out=minus_mean_of[g][:, pair], in0=mean_var[:, pair, 0], scalar1=-1.0, scalar2=0.0, op0=ALU.mult, op1=ALU.add
             )
-            rstd_of[g] = rstd
-            minus_mean_of[g] = minus_mean
+            if g == 0:
+                nc.gpsimd.tensor_tensor(
+                    out=shift_of[g][:, pair], in0=minus_mean_of[g][:, pair], in1=rstd_of[g][:, pair], op=ALU.mult
+                )
 
         def normalise(g, j):
             if j == 0:
                 x_hat = hats.tile([P, TILES, D], F32)
                 x_hat_of[g] = x_hat
-            nc.gpsimd.tensor_scalar(
-                out=x_hat_of[g][:, j, :],
-                in0=x_of[g][:, j, :],
-                scalar1=minus_mean_of[g][:, j : j + 1],
-                scalar2=rstd_of[g][:, j : j + 1],
-                op0=ALU.add,
-                op1=ALU.mult,
-            )
+            if g == 0:
+                nc.scalar.activation(
+                    out=x_hat_of[g][:, j, :],
+                    in_=x_of[g][:, j, :],
+                    func=ACT.Identity,
+                    scale=rstd_of[g][:, j : j + 1],
+                    bias=shift_of[g][:, j : j + 1],
+                )
+            else:
+                nc.gpsimd.tensor_scalar(
+                    out=x_hat_of[g][:, j, :],
+                    in0=x_of[g][:, j, :],
+                    scalar1=minus_mean_of[g][:, j : j + 1],
+                    scalar2=rstd_of[g][:, j : j + 1],
+                    op0=ALU.add,
+                    op1=ALU.mult,
+                )
 
         def transpose_chunk(g, c):
             s, t = divmod(c, PACK)
@@ -239,19 +259,19 @@ def tile_efficientcrossattention_pa_t_kernel(tc, x, ln_w, ln_b, q_w, q_b, out):
 
         def divide(g, j):
             result = result_of[g]
+            scalar_heads = 3 if j % 2 == 0 else 2
             for h in range(HEADS):
-                if j < SCALAR_TILES:
+                if h < scalar_heads:
                     nc.scalar.activation(
                         out=result[:, j, h, :], in_=result[:, j, h, :], func=ACT.Copy, scale=inv_of[g][:, j, h : h + 1]
                     )
                 else:
-                    nc.gpsimd.tensor_scalar(
+                    nc.vector.tensor_scalar(
                         out=result[:, j, h, :],
                         in0=result[:, j, h, :],
                         scalar1=inv_of[g][:, j, h : h + 1],
-                        scalar2=0.0,
+                        scalar2=None,
                         op0=ALU.mult,
-                        op1=ALU.add,
                     )
 
         def store(g, j):
@@ -277,15 +297,10 @@ def tile_efficientcrossattention_pa_t_kernel(tc, x, ln_w, ln_b, q_w, q_b, out):
             else:
                 quantise(g, r // 2)
 
-        def divide_two(g, r):
-            if r < SCALAR_TILES:
-                divide(g, r)
-                divide(g, r + SCALAR_TILES)
-
-        def store_two(g, r):
-            if r < SCALAR_TILES:
-                store(g, r)
-                store(g, r + SCALAR_TILES)
+        def scalars_and_normalise(g, j):
+            if j % 2 == 0:
+                token_scalars(g, j // 2)
+            normalise(g, j)
 
         def tick(t):
             piece(load, t + 13)
@@ -297,13 +312,14 @@ def tile_efficientcrossattention_pa_t_kernel(tc, x, ln_w, ln_b, q_w, q_b, out):
             whole(invert_sums, t - 18)
             piece(statistics, t + 9)
             piece(exponentials, t - 14)
-            whole(token_scalars, t + 5)
-            piece(normalise, t + 5)
+            piece(scalars_and_normalise, t + 7)
             piece(divide, t - 19)
             piece(store, t - 20)
 
         for t in range(-13, 4 * (GROUPS - 1) + 24):
             tick(t)
+            if t == -10:
+                nc.scalar.dma_start(out=w_rows[:], in_=q_w.rearrange("(c p) n -> p c n", p=P))
             if t == -6:
                 transpose_norm_constants()
             if t == -2:

from contextlib import ExitStack

import concourse.mybir as mybir
from concourse.masks import make_identity

F32 = mybir.dt.float32
BF16 = mybir.dt.bfloat16
U32 = mybir.dt.uint32
U8 = mybir.dt.uint8
FP8X4 = mybir.dt.float8_e4m3fn_x4
ALU = mybir.AluOpType
ACT = mybir.ActivationFunctionType
AXIS = mybir.AxisListType

P = 128
PACK = 4
TOKENS = 8 * 1024
D = 1024
A = 512
HEADS = 4
HEAD = A // HEADS
CHUNKS = D // P
PASSES = D // (P * PACK)
TILES = 4
GROUP = TILES * P
GROUPS = TOKENS // GROUP
BN_MAX = 512
BN_PARTS = D // BN_MAX
RUN = 4
EPS = 1e-5

FLOPS = 2 * TOKENS * D * A


def tile_efficientcrossattention_pa_t_kernel(tc, x, ln_w, ln_b, q_w, q_b, out):
    nc = tc.nc
    x_groups = x.flatten_outer_dims().rearrange("(g j p) k -> g j p k", p=P, j=TILES)
    out_groups = out.flatten_outer_dims().rearrange("(g j p) a -> g j p a", p=P, j=TILES)

    with ExitStack() as stack:
        const = stack.enter_context(tc.tile_pool(name="const", bufs=1))
        loads = stack.enter_context(tc.tile_pool(name="loads", bufs=5))
        small = stack.enter_context(tc.tile_pool(name="small", bufs=4))
        hats = stack.enter_context(tc.tile_pool(name="hats", bufs=3))
        plane_pool = stack.enter_context(tc.tile_pool(name="plane_pool", bufs=2 * PASSES))
        packed = stack.enter_context(tc.tile_pool(name="packed", bufs=3))
        logit_pool = stack.enter_context(tc.tile_pool(name="logit_pool", bufs=3))
        stores = stack.enter_context(tc.tile_pool(name="stores", bufs=4))
        psum_t = stack.enter_context(tc.psum_pool(name="psum_t", bufs=2))
        psum_q = stack.enter_context(tc.psum_pool(name="psum_q", bufs=2))
        psum_l = stack.enter_context(tc.psum_pool(name="psum_l", bufs=TILES))
        stack.enter_context(tc.manual_schedule())

        ln_rows = const.tile([P, P], BF16)
        nc.vector.memset(ln_rows[:], 0.0)
        nc.sync.dma_start(out=ln_rows[0:CHUNKS, :], in_=ln_w.rearrange("(c p) -> c p", p=P))
        nc.sync.dma_start(out=ln_rows[CHUNKS : 2 * CHUNKS, :], in_=ln_b.rearrange("(c p) -> c p", p=P))
        nc.sync.dma_start(out=ln_rows[2 * CHUNKS : 2 * CHUNKS + HEADS, :], in_=q_b.rearrange("(h p) -> h p", p=P))
        w_rows = const.tile([P, CHUNKS, A], BF16)

        identity = const.tile([P, P], F32)
        make_identity(nc, identity[:])
        minus_half = const.tile([P, TILES], F32)
        nc.gpsimd.memset(minus_half[:], -0.5)

        ln_cols = const.tile([P, 2 * CHUNKS + HEADS], F32)

        def transpose_norm_constants():
            ln_rows_f32 = const.tile([P, P], F32)
            nc.vector.tensor_copy(out=ln_rows_f32[:], in_=ln_rows[:])
            ln_bank = psum_t.tile([P, GROUP], F32, tag="xt")
            nc.tensor.transpose(out=ln_bank[:, 0:P], in_=ln_rows_f32[:], identity=identity[:])
            nc.vector.tensor_copy(out=ln_cols[:], in_=ln_bank[:, 0 : 2 * CHUNKS + HEADS])

        w_codes = const.tile([P, PASSES, A], U32, align_bytes=64)
        w_scales = const.tile([P, PASSES, A], U8, align_bytes=64)

        def quantise_weights():
            w_grouped = const.tile([P, PASSES, A, PACK], BF16, align_bytes=64)
            for s in range(PASSES):
                nc.vector.tensor_copy(
                    out=w_grouped[:, s].rearrange("p (c i) t -> p c t i", i=RUN),
                    in_=w_rows[:, s * PACK : (s + 1) * PACK, :].rearrange("p t (c i) -> p c t i", i=RUN),
                )
            nc.vector.quantize_mx(
                out=w_codes[:].rearrange("p s n -> p (s n)").bitcast(FP8X4),
                scales=w_scales[:].rearrange("p s n -> p (s n)"),
                in_=w_grouped[:].rearrange("p s n t -> p (s n t)"),
            )

        shift_of, var_eps_of = {}, {}
        x_of, stats_of, mean_var_of, rstd_of, minus_mean_of, x_hat_of, planes_of, grouped_of = {}, {}, {}, {}, {}, {}, {}, {}
        codes_of, scales_of, logits_t_of, logits_of, minus_max_of, result_of, sums_of, inv_of = {}, {}, {}, {}, {}, {}, {}, {}

        def load(g, j):
            if j == 0:
                x_sb = loads.tile([P, TILES, D], BF16)
                x_of[g] = x_sb
            nc.scalar.dma_start(out=x_of[g][:, j, :], in_=x_groups[g, j])

        def statistics(g, j):
            if j == 0:
                stats = small.tile([P, TILES, BN_PARTS, 6], F32)
                mean_var = small.tile([P, TILES, 2], F32)
                stats_of[g] = stats
                mean_var_of[g] = mean_var
            for h in range(BN_PARTS):
                nc.vector.bn_stats(out=stats_of[g][:, j, h, :], in_=x_of[g][:, j, h * BN_MAX : (h + 1) * BN_MAX])
            if j % 2 == 1:
                for i in (j - 1, j):
                    nc.vector.bn_aggr(out=mean_var_of[g][:, i, :], in_=stats_of[g][:, i].rearrange("p h s -> p (h s)"))

        def token_scalars(g, half):
            if half == 0:
                var_eps = small.tile([P, TILES], F32)
                rstd = small.tile([P, TILES], F32)
                minus_mean = small.tile([P, TILES], F32)
                var_eps_of[g] = var_eps
                rstd_of[g] = rstd
                minus_mean_of[g] = minus_mean
                if g == 0:
                    shift = small.tile([P, TILES], F32)
                    shift_of[g] = shift
            pair = slice(2 * half, 2 * half + 2)
            mean_var = mean_var_of[g]
            nc.gpsimd.tensor_scalar(
                out=var_eps_of[g][:, pair], in0=mean_var[:, pair, 1], scalar1=1.0, scalar2=EPS, op0=ALU.mult, op1=ALU.add
            )
            nc.gpsimd.tensor_tensor(out=rstd_of[g][:, pair], in0=var_eps_of[g][:, pair], in1=minus_half[:, pair], op=ALU.pow)
            nc.gpsimd.tensor_scalar(
                out=minus_mean_of[g][:, pair], in0=mean_var[:, pair, 0], scalar1=-1.0, scalar2=0.0, op0=ALU.mult, op1=ALU.add
            )
            if g == 0:
                nc.gpsimd.tensor_tensor(
                    out=shift_of[g][:, pair], in0=minus_mean_of[g][:, pair], in1=rstd_of[g][:, pair], op=ALU.mult
                )

        def normalise(g, j):
            if j == 0:
                x_hat = hats.tile([P, TILES, D], F32)
                x_hat_of[g] = x_hat
            if g == 0:
                nc.scalar.activation(
                    out=x_hat_of[g][:, j, :],
                    in_=x_of[g][:, j, :],
                    func=ACT.Identity,
                    scale=rstd_of[g][:, j : j + 1],
                    bias=shift_of[g][:, j : j + 1],
                )
            else:
                nc.gpsimd.tensor_scalar(
                    out=x_hat_of[g][:, j, :],
                    in0=x_of[g][:, j, :],
                    scalar1=minus_mean_of[g][:, j : j + 1],
                    scalar2=rstd_of[g][:, j : j + 1],
                    op0=ALU.add,
                    op1=ALU.mult,
                )

        def transpose_chunk(g, c):
            s, t = divmod(c, PACK)
            if t == 0:
                planes = plane_pool.tile([P, PACK, GROUP], BF16)
                planes_of[g, s] = planes
            xt = psum_t.tile([P, GROUP], F32, tag="xt")
            for j in range(TILES):
                nc.tensor.transpose(
                    out=xt[:, j * P : (j + 1) * P],
                    in_=x_hat_of[g][:, j, c * P : (c + 1) * P],
                    identity=identity[:],
                )
            nc.scalar.activation(
                out=planes_of[g, s][:, t, :],
                in_=xt[:],
                func=ACT.Identity,
                scale=ln_cols[:, c : c + 1],
                bias=ln_cols[:, CHUNKS + c : CHUNKS + c + 1],
            )

        def regroup(g, s):
            grouped = packed.tile([P, GROUP, PACK], BF16, align_bytes=64)
            nc.vector.tensor_copy(
                out=grouped[:].rearrange("p (c i) t -> p c t i", i=RUN),
                in_=planes_of[g, s][:].rearrange("p t (c i) -> p c t i", i=RUN),
            )
            grouped_of[g, s] = grouped

        def quantise(g, s):
            if s == 0:
                codes = packed.tile([P, PASSES, GROUP], U32, align_bytes=64)
                scales = packed.tile([P, PASSES, GROUP], U8, align_bytes=64)
                codes_of[g] = codes
                scales_of[g] = scales
            nc.vector.quantize_mx(
                out=codes_of[g][:, s, :].bitcast(FP8X4),
                scales=scales_of[g][:, s, :],
                in_=grouped_of[g, s][:].rearrange("p w t -> p (w t)"),
            )

        def project(g, h):
            if h == 0:
                logits_t = logit_pool.tile([P, HEADS, GROUP], F32)
                logits_t_of[g] = logits_t
            acc = psum_q.tile([P, GROUP], F32)
            for s in range(PASSES):
                nc.tensor.matmul_mx(
                    out=acc[:],
                    lhsT=w_codes[:, s, h * HEAD : (h + 1) * HEAD].bitcast(FP8X4),
                    lhsT_scale=w_scales[:, s, h * HEAD : (h + 1) * HEAD],
                    rhs=codes_of[g][:, s, :].bitcast(FP8X4),
                    rhs_scale=scales_of[g][:, s, :],
                    start=(s == 0),
                    stop=(s == PASSES - 1),
                )
            nc.scalar.activation(
                out=logits_t_of[g][:, h, :],
                in_=acc[:],
                func=ACT.Identity,
                scale=1.0,
                bias=ln_cols[:, 2 * CHUNKS + h : 2 * CHUNKS + h + 1],
            )

        def transpose_back(g, j):
            logits = psum_l.tile([P, HEADS, HEAD], F32)
            for h in range(HEADS):
                nc.tensor.transpose(
                    out=logits[:, h, :], in_=logits_t_of[g][:, h, j * P : (j + 1) * P], identity=identity[:]
                )
            logits_of[g, j] = logits

        def find_max(g, j):
            if j == 0:
                minus_max = small.tile([P, TILES, HEADS], F32)
                minus_max_of[g] = minus_max
            nc.vector.tensor_reduce(
                out=minus_max_of[g][:, j, :], in_=logits_of[g, j][:], axis=AXIS.X, op=ALU.max, negate=True
            )

        def exponentials(g, j):
            if j == 0:
                result = stores.tile([P, TILES, HEADS, HEAD], F32)
                sums = small.tile([P, TILES, HEADS], F32)
                result_of[g] = result
                sums_of[g] = sums
            for h in range(HEADS):
                nc.scalar.activation(
                    out=result_of[g][:, j, h, :],
                    in_=logits_of[g, j][:, h, :],
                    func=ACT.Exp,
                    bias=minus_max_of[g][:, j, h : h + 1],
                    scale=1.0,
                    accum_out=sums_of[g][:, j, h : h + 1],
                )

        def invert_sums(g):
            inv_sums = small.tile([P, TILES, HEADS], F32)
            nc.vector.reciprocal(out=inv_sums[:], in_=sums_of[g][:])
            inv_of[g] = inv_sums

        def divide(g, j):
            result = result_of[g]
            scalar_heads = 3 if j % 2 == 0 else 2
            for h in range(HEADS):
                if h < scalar_heads:
                    nc.scalar.activation(
                        out=result[:, j, h, :], in_=result[:, j, h, :], func=ACT.Copy, scale=inv_of[g][:, j, h : h + 1]
                    )
                else:
                    nc.vector.tensor_scalar(
                        out=result[:, j, h, :],
                        in0=result[:, j, h, :],
                        scalar1=inv_of[g][:, j, h : h + 1],
                        scalar2=None,
                        op0=ALU.mult,
                    )

        def store(g, j):
            nc.sync.dma_start(out=out_groups[g, j], in_=result_of[g][:, j].rearrange("p h a -> p (h a)"))

        def piece(stage, index):
            g, r = divmod(index, TILES)
            if 0 <= g < GROUPS:
                stage(g, r)

        def whole(stage, index):
            g, r = divmod(index, TILES)
            if r == 0 and 0 <= g < GROUPS:
                stage(g)

        def two_chunks(g, r):
            transpose_chunk(g, 2 * r)
            transpose_chunk(g, 2 * r + 1)

        def regroup_or_quantise(g, r):
            if r % 2 == 0:
                regroup(g, r // 2)
            else:
                quantise(g, r // 2)

        def scalars_and_normalise(g, j):
            if j % 2 == 0:
                token_scalars(g, j // 2)
            normalise(g, j)

        def tick(t):
            piece(load, t + 13)
            piece(two_chunks, t)
            piece(project, t - 8)
            piece(transpose_back, t - 12)
            piece(find_max, t - 13)
            piece(regroup_or_quantise, t - 3)
            whole(invert_sums, t - 18)
            piece(statistics, t + 9)
            piece(exponentials, t - 14)
            piece(scalars_and_normalise, t + 7)
            piece(divide, t - 19)
            piece(store, t - 20)

        for t in range(-13, 4 * (GROUPS - 1) + 24):
            tick(t)
            if t == -10:
                nc.scalar.dma_start(out=w_rows[:], in_=q_w.rearrange("(c p) n -> p c n", p=P))
            if t == -6:
                transpose_norm_constants()
            if t == -2:
                quantise_weights()
